import numpy as np
import ml_dtypes


def mxq(x, axis, fmt="e4m3"):
    dtype, down = {"e4m3": (ml_dtypes.float8_e4m3fn, 7), "e5m2": (ml_dtypes.float8_e5m2, 14)}[fmt]
    v = np.moveaxis(np.asarray(x, np.float32).astype(ml_dtypes.bfloat16).astype(np.float64), axis, -1)
    blocks = v.reshape(v.shape[:-1] + (-1, 32))
    amax = np.abs(blocks).max(-1, keepdims=True)
    byte = np.maximum(np.where(amax > 0, np.frexp(amax)[1] - 1 + 127, 0) - down, 1)
    scale = np.exp2(byte - 127.0)
    codes = (blocks / scale).astype(np.float32).astype(dtype).astype(np.float64)
    return np.moveaxis((codes * scale).reshape(v.shape), -1, axis)


WIDE = False


def mx_kscale(k):
    if not WIDE:
        return np.ones(k)
    levels = np.array([10, -10, 5, -5, 0])
    if k % 512:
        return np.exp2(np.random.permutation(np.resize(levels, k // 32))).repeat(32)
    a = np.empty((k // 512, 16))
    for p in range(k // 512):
        a[p, :8] = np.random.permutation(np.resize(levels, 8))
        for g in range(8):
            far = levels[np.abs(levels - a[p, g]) >= 10]
            a[p, g + 8] = far[np.random.randint(len(far))]
    return np.exp2(a.ravel()).repeat(32)


BF16 = ml_dtypes.bfloat16


def bf(x):
    return np.asarray(x, np.float32).astype(BF16)


def f64(x):
    return np.asarray(x).astype(np.float64)


B, HH, WW, C, NH, KD, WS, SS = 1, 64, 64, 512, 8, 64, 8, 4
GH, GW, T, F = HH // WS, WW // WS, WS * WS, NH * KD
N = B * GH * GW


def setup_inputs():
    s = mx_kscale(C)

    def weight():
        return bf(np.random.standard_normal((C, NH, KD)) / np.sqrt(C) / s[:, None, None])

    def bias():
        return bf(np.random.standard_normal((NH, KD)) * 0.3)

    return {"x": bf(np.random.standard_normal((B, HH, WW, C)) * s), "wq": weight(), "bq": bias(),
            "wk": weight(), "bk": bias(), "wv": weight(), "bv": bias()}


def reference(x, wq, bq, wk, bk, wv, bv):
    shifted = np.roll(f64(x), shift=(-SS, -SS), axis=(1, 2))
    win = shifted.reshape(B, GH, WS, GW, WS, C).swapaxes(2, 3).reshape(N * T, C)
    wn = mxq(win, 1, "e4m3")
    q = (wn @ mxq(f64(wq).reshape(C, F), 0, "e4m3")).reshape(N, T, NH, KD) + f64(bq)
    k = (wn @ mxq(f64(wk).reshape(C, F), 0, "e4m3")).reshape(N, T, NH, KD) + f64(bk)
    v = (wn @ mxq(f64(wv).reshape(C, F), 0, "e4m3")).reshape(N, T, NH, KD) + f64(bv)
    return q, k, v

@@ -1,0 +1,240 @@
+from contextlib import ExitStack
+
+import concourse.mybir as mybir
+from concourse.masks import make_identity
+
+F32 = mybir.dt.float32
+BF16 = mybir.dt.bfloat16
+U32 = mybir.dt.uint32
+U8 = mybir.dt.uint8
+FP8X4 = mybir.dt.float8_e4m3fn_x4
+ADD = mybir.AluOpType.add
+IDENTITY = mybir.ActivationFunctionType.Identity
+
+P = 128
+F = 512
+FLOPS = 2 * 4096 * 512 * 1536
+
+
+def tile_windowattentionblock_pa_kernel(tc, x, wq, bq, wk, bk, wv, bv, out_0, out_1, out_2):
+    nc = tc.nc
+    weights = (wq, wk, wv)
+    biases = (bq, bk)
+    x_rows = x.rearrange("b r (cb cl) c -> (b r cb) (cl c)", cl=8)
+    out_blocks = [
+        o.rearrange("(g n) (ti tj) h d -> g (n ti) (tj h d)", g=4, tj=8) for o in (out_0, out_1, out_2)
+    ]
+
+    with ExitStack() as ctx:
+        const = ctx.enter_context(tc.tile_pool(name="const", bufs=1))
+        xq = ctx.enter_context(tc.tile_pool(name="xq", bufs=2))
+        flip = ctx.enter_context(tc.tile_pool(name="flip", bufs=2))
+        stage = ctx.enter_context(tc.tile_pool(name="stage", bufs=5))
+        psum = ctx.enter_context(tc.psum_pool(name="psum", bufs=1))
+        ctx.enter_context(tc.manual_schedule())
+
+        ident = const.tile([P, P], F32, name="ident")
+        ident_bf = const.tile([P, P], BF16, name="ident_bf")
+        perm_a = const.tile([P, P], F32, name="perm_a")
+        perm_b = const.tile([P, P], F32, name="perm_b")
+        ones = const.tile([P, P], BF16, name="ones")
+        bias_rows = const.tile([P, 2 * F], BF16, name="bias_rows")
+        bias_v_rows = const.tile([P, P], BF16, name="bias_v_rows")
+        bias_all = const.tile([P, 2, F], F32, name="bias_all")
+        bias_col = const.tile([P, 4], F32, name="bias_col")
+        w_raw = [const.tile([P, 4, F], BF16, name="w_raw%d" % o) for o in range(3)]
+        w_grp = [const.tile([P, F, 4], BF16, name="w_grp%d" % o, align_bytes=64) for o in range(3)]
+        w_codes = [const.tile([P, F], U32, name="w_codes%d" % o, align_bytes=64) for o in range(3)]
+        w_scales = [const.tile([P, F], U8, name="w_scales%d" % o, align_bytes=64) for o in range(3)]
+        x_sb = [const.tile([P, 8 * F], BF16, name="x_sb%d" % g) for g in range(4)]
+
+        def load_w(o):
+            nc.sync.dma_start(
+                out=w_raw[o][:].rearrange("q t f -> q (t f)"),
+                in_=weights[o].rearrange("(q t) h d -> q (t h d)", t=4),
+            )
+
+        def load_b(o):
+            nc.sync.dma_start(
+                out=bias_rows[0:1, o * F : (o + 1) * F], in_=biases[o].rearrange("(o h) d -> o (h d)", o=1)
+            )
+
+        def load_x(blk, c0, c1):
+            r0 = (16 * blk + 4) * 8
+            n = min(P, 512 - r0)
+            nc.sync.dma_start(out=x_sb[blk][0:n, c0:c1], in_=x_rows[r0 : r0 + n, c0:c1])
+            if n < P:
+                nc.sync.dma_start(out=x_sb[blk][n:P, c0:c1], in_=x_rows[0 : P - n, c0:c1])
+
+        nc.vector.memset(bias_rows[:].bitcast(F32), 0.0)
+        nc.vector.memset(bias_v_rows[:].bitcast(F32), 0.0)
+        nc.vector.memset(ones[:], 1.0)
+        make_identity(nc, ident[:])
+        make_identity(nc, ident_bf[:])
+
+        load_x(0, 4 * F, 8 * F)
+        load_b(0)
+        load_w(0)
+        load_w(2)
+        nc.sync.dma_start(out=bias_v_rows[0:4, :], in_=bv.rearrange("(c h) d -> c (h d)", c=4))
+        load_b(1)
+        load_w(1)
+        load_x(0, 0, 4 * F)
+        load_x(1, 0, 8 * F)
+        load_x(2, 0, 8 * F)
+        load_x(3, 0, 8 * F)
+
+        src = ident[:].rearrange("k (a t g) -> k a g t", a=2, t=8, g=8)
+        nc.vector.tensor_copy(out=perm_a[:].rearrange("k (a g t) -> k a g t", a=2, g=8, t=8), in_=src)
+        dst_b = perm_b[:].rearrange("k (a g t) -> k a g t", a=2, g=8, t=8)
+        nc.vector.tensor_copy(out=dst_b[:, :, 0:7, :], in_=src[:, :, 1:8, :])
+        nc.vector.tensor_copy(out=dst_b[:, :, 7:8, :], in_=src[:, :, 0:1, :])
+
+        def spread_bias(o):
+            bank = psum.tile([P, F], F32, tag="at", bufs=2, name="bank")
+            nc.tensor.matmul(out=bank[:], lhsT=ones[:], rhs=bias_rows[:, o * F : (o + 1) * F], start=True, stop=True)
+            nc.scalar.copy(out=bias_all[:, o, :], in_=bank[:])
+
+        def stand_bias_v():
+            bank = psum.tile([P, F], F32, tag="at", bufs=2, name="bank")
+            nc.tensor.matmul(out=bank[:, 0:32], lhsT=bias_v_rows[:], rhs=ident_bf[:, 0:32], start=True, stop=True)
+            nc.scalar.copy(out=bias_col[:], in_=bank[:, 0:4])
+
+        def regroup_w(o, engine_copy):
+            engine_copy(
+                out=w_grp[o][:].rearrange("p (c i) t -> p c t i", i=4),
+                in_=w_raw[o][:].rearrange("p t (c i) -> p c t i", i=4),
+            )
+
+        def quant_w(o):
+            nc.vector.quantize_mx(
+                out=w_codes[o][:].bitcast(FP8X4),
+                scales=w_scales[o][:],
+                in_=w_grp[o][:].rearrange("p f t -> p (f t)"),
+            )
+
+        grouped = {}
+        packed = {}
+        staged = {}
+        flipped = {}
+
+        def transposes(g):
+            blk, half = divmod(g, 2)
+            perm = perm_a if half == 0 else perm_b
+            words = x_sb[blk][:].bitcast(F32)
+            gx = xq.tile([P, 4 * F], BF16, tag="gx", name="gx", align_bytes=64)
+            gw = gx[:].bitcast(F32)
+            for b in range(2):
+                xt = psum.tile([P, F], F32, tag="t", bufs=3, name="xt")
+                for s in range(2):
+                    cl = (4 if half == 0 else 0) + 2 * b + s
+                    for u in range(2):
+                        j = 2 * s + u
+                        c0 = cl * 256 + u
+                        nc.tensor.transpose(xt[:, j * P : (j + 1) * P], words[:, c0 : c0 + 255 : 2], perm[:])
+                nc.scalar.copy(
+                    out=gw[:, b * F : (b + 1) * F].rearrange("p (s n u) -> p s n u", s=2, u=2),
+                    in_=xt[:].rearrange("p (s u n) -> p s n u", s=2, u=2),
+                )
+            grouped[g] = gx
+
+        def quant_x(g):
+            codes = xq.tile([P, F], U32, tag="xc", name="codes", align_bytes=64)
+            scales = xq.tile([P, F], U8, tag="xs", name="scales", align_bytes=64)
+            nc.vector.quantize_mx(out=codes[:].bitcast(FP8X4), scales=scales[:], in_=grouped[g][:])
+            packed[g] = (codes, scales)
+
+        def store(g, o, s0, s1):
+            blk, half = divmod(g, 2)
+            c0 = half * 4 * F
+            nc.sync.dma_start(
+                out=out_blocks[o][blk][:, c0 + s0 * F : c0 + s1 * F], in_=staged[(g, o)][:, s0 * F : s1 * F]
+            )
+
+        def vector_bank(g, o, s):
+            if s == 0:
+                staged[(g, o)] = stage.tile([P, 4 * F], F32, tag="st%d" % o, name="st%d" % o)
+            codes, scales = packed[g]
+            cols = slice(s * P, (s + 1) * P)
+            acc = psum.tile([P, F], F32, tag="av", bufs=3, name="acc_v")
+            nc.tensor.matmul_mx(
+                out=acc[:],
+                lhsT=codes[:, cols].bitcast(FP8X4),
+                lhsT_scale=scales[:, cols],
+                rhs=w_codes[o][:].bitcast(FP8X4),
+                rhs_scale=w_scales[o][:],
+                start=True,
+                stop=True,
+            )
+            nc.vector.tensor_tensor(
+                out=staged[(g, o)][:, s * F : (s + 1) * F], in0=acc[:], in1=bias_all[:, o, :], op=ADD
+            )
+            if s == 3:
+                store(g, o, 0, 4)
+
+        def channel_bank(g, c):
+            codes, scales = packed[g]
+            cols = slice(c * P, (c + 1) * P)
+            acc = psum.tile([P, F], F32, tag="at", bufs=2, name="acc_t")
+            nc.tensor.matmul_mx(
+                out=acc[:],
+                lhsT=w_codes[2][:, cols].bitcast(FP8X4),
+                lhsT_scale=w_scales[2][:, cols],
+                rhs=codes[:].bitcast(FP8X4),
+                rhs_scale=scales[:],
+                start=True,
+                stop=True,
+            )
+            vt = flip.tile([P, F], F32, tag="vt%d" % c, name="vt%d" % c)
+            nc.scalar.activation(out=vt[:], in_=acc[:], func=IDENTITY, bias=bias_col[:, c : c + 1], scale=1.0)
+            flipped[(g, c)] = vt
+
+        def flip_back(g, s, engine_copy):
+            if s == 0:
+                staged[(g, 2)] = stage.tile([P, 4 * F], F32, tag="st2", name="st2")
+            bank = psum.tile([P, F], F32, tag="t", bufs=3, name="bk")
+            for c in range(4):
+                nc.tensor.transpose(bank[:, c * P : (c + 1) * P], flipped[(g, c)][:, s * P : (s + 1) * P], ident[:])
+            engine_copy(out=staged[(g, 2)][:, s * F : (s + 1) * F], in_=bank[:])
+
+        transposes(0)
+        regroup_w(0, nc.vector.tensor_copy)
+        quant_w(0)
+        spread_bias(0)
+        quant_x(0)
+        regroup_w(2, nc.scalar.copy)
+        regroup_w(1, nc.scalar.copy)
+        stand_bias_v()
+        spread_bias(1)
+
+        for g in range(8):
+            vector_bank(g, 0, 0)
+            vector_bank(g, 0, 1)
+            if g == 0:
+                quant_w(2)
+            channel_bank(g, 0)
+            vector_bank(g, 0, 2)
+            channel_bank(g, 1)
+            vector_bank(g, 0, 3)
+            if g < 7:
+                transposes(g + 1)
+            if g > 0:
+                flip_back(g - 1, 0, nc.scalar.copy)
+            if g == 0:
+                quant_w(1)
+            vector_bank(g, 1, 0)
+            if g < 7:
+                quant_x(g + 1)
+            vector_bank(g, 1, 1)
+            channel_bank(g, 2)
+            vector_bank(g, 1, 2)
+            channel_bank(g, 3)
+            vector_bank(g, 1, 3)
+            if g > 0:
+                for s in range(1, 4):
+                    flip_back(g - 1, s, nc.scalar.copy)
+                store(g - 1, 2, 0, 4)
+        for s in range(4):
+            flip_back(7, s, nc.vector.tensor_copy if s % 2 == 0 else nc.scalar.copy)
+            if s % 2 == 1:
+                store(7, 2, s - 1, s + 1)

@@ -72,13 +72,14 @@ def tile_windowattentionblock_pa_kernel(tc, x, wq, bq, wk, bk, wv, bv, out_0, ou
         make_identity(nc, ident[:])
         make_identity(nc, ident_bf[:])
 
-        load_x(0, 4 * F, 8 * F)
-        load_b(0)
         load_w(0)
+        load_b(0)
+        load_x(0, 4 * F, 6 * F)
+        load_x(0, 6 * F, 8 * F)
+        load_w(1)
+        load_b(1)
         load_w(2)
         nc.sync.dma_start(out=bias_v_rows[0:4, :], in_=bv.rearrange("(c h) d -> c (h d)", c=4))
-        load_b(1)
-        load_w(1)
         load_x(0, 0, 4 * F)
         load_x(1, 0, 8 * F)
         load_x(2, 0, 8 * F)
@@ -118,13 +119,14 @@ def tile_windowattentionblock_pa_kernel(tc, x, wq, bq, wk, bk, wv, bv, out_0, ou
         staged = {}
         flipped = {}
 
-        def transposes(g):
+        def transposes(g, pairs=(0, 1)):
             blk, half = divmod(g, 2)
             perm = perm_a if half == 0 else perm_b
             words = x_sb[blk][:].bitcast(F32)
-            gx = xq.tile([P, 4 * F], BF16, tag="gx", name="gx", align_bytes=64)
-            gw = gx[:].bitcast(F32)
-            for b in range(2):
+            if 0 in pairs:
+                grouped[g] = xq.tile([P, 4 * F], BF16, tag="gx", name="gx", align_bytes=64)
+            gw = grouped[g][:].bitcast(F32)
+            for b in pairs:
                 xt = psum.tile([P, F], F32, tag="t", bufs=3, name="xt")
                 for s in range(2):
                     cl = (4 if half == 0 else 0) + 2 * b + s
@@ -136,13 +138,18 @@ def tile_windowattentionblock_pa_kernel(tc, x, wq, bq, wk, bk, wv, bv, out_0, ou
                     out=gw[:, b * F : (b + 1) * F].rearrange("p (s n u) -> p s n u", s=2, u=2),
                     in_=xt[:].rearrange("p (s u n) -> p s n u", s=2, u=2),
                 )
-            grouped[g] = gx
 
-        def quant_x(g):
-            codes = xq.tile([P, F], U32, tag="xc", name="codes", align_bytes=64)
-            scales = xq.tile([P, F], U8, tag="xs", name="scales", align_bytes=64)
-            nc.vector.quantize_mx(out=codes[:].bitcast(FP8X4), scales=scales[:], in_=grouped[g][:])
-            packed[g] = (codes, scales)
+        def quant_x(g, s0=0, s1=4):
+            if s0 == 0:
+                codes = xq.tile([P, F], U32, tag="xc", name="codes", align_bytes=64)
+                scales = xq.tile([P, F], U8, tag="xs", name="scales", align_bytes=64)
+                packed[g] = (codes, scales)
+            codes, scales = packed[g]
+            nc.vector.quantize_mx(
+                out=codes[:, s0 * P : s1 * P].bitcast(FP8X4),
+                scales=scales[:, s0 * P : s1 * P],
+                in_=grouped[g][:, s0 * F : s1 * F],
+            )
 
         def store(g, o, s0, s1):
             blk, half = divmod(g, 2)
@@ -197,31 +204,38 @@ def tile_windowattentionblock_pa_kernel(tc, x, wq, bq, wk, bk, wv, bv, out_0, ou
                 nc.tensor.transpose(bank[:, c * P : (c + 1) * P], flipped[(g, c)][:, s * P : (s + 1) * P], ident[:])
             engine_copy(out=staged[(g, 2)][:, s * F : (s + 1) * F], in_=bank[:])
 
-        transposes(0)
+        spread_bias(0)
+        transposes(0, (0,))
+        transposes(0, (1,))
         regroup_w(0, nc.vector.tensor_copy)
         quant_w(0)
-        spread_bias(0)
-        quant_x(0)
-        regroup_w(2, nc.scalar.copy)
+        quant_x(0, 0, 2)
+        quant_x(0, 2, 4)
         regroup_w(1, nc.scalar.copy)
-        stand_bias_v()
+        for s in range(4):
+            vector_bank(0, 0, s)
         spread_bias(1)
+        transposes(1)
+        quant_w(1)
+        for s in range(4):
+            vector_bank(0, 1, s)
+        regroup_w(2, nc.scalar.copy)
+        stand_bias_v()
+        quant_x(1)
+        quant_w(2)
+        for c in range(4):
+            channel_bank(0, c)
 
-        for g in range(8):
+        for g in range(1, 8):
             vector_bank(g, 0, 0)
             vector_bank(g, 0, 1)
-            if g == 0:
-                quant_w(2)
             channel_bank(g, 0)
             vector_bank(g, 0, 2)
             channel_bank(g, 1)
             vector_bank(g, 0, 3)
             if g < 7:
                 transposes(g + 1)
-            if g > 0:
-                flip_back(g - 1, 0, nc.scalar.copy)
-            if g == 0:
-                quant_w(1)
+            flip_back(g - 1, 0, nc.scalar.copy)
             vector_bank(g, 1, 0)
             if g < 7:
                 quant_x(g + 1)
@@ -230,10 +244,9 @@ def tile_windowattentionblock_pa_kernel(tc, x, wq, bq, wk, bk, wv, bv, out_0, ou
             vector_bank(g, 1, 2)
             channel_bank(g, 3)
             vector_bank(g, 1, 3)
-            if g > 0:
-                for s in range(1, 4):
-                    flip_back(g - 1, s, nc.scalar.copy)
-                store(g - 1, 2, 0, 4)
+            for s in range(1, 4):
+                flip_back(g - 1, s, nc.scalar.copy)
+            store(g - 1, 2, 0, 4)
         for s in range(4):
             flip_back(7, s, nc.vector.tensor_copy if s % 2 == 0 else nc.scalar.copy)
             if s % 2 == 1:

@@ -19,7 +19,7 @@ FLOPS = 2 * 4096 * 512 * 1536
 def tile_windowattentionblock_pa_kernel(tc, x, wq, bq, wk, bk, wv, bv, out_0, out_1, out_2):
     nc = tc.nc
     weights = (wq, wk, wv)
-    biases = (bq, bk)
+    biases = (bq, bk, bv)
     x_rows = x.rearrange("b r (cb cl) c -> (b r cb) (cl c)", cl=8)
     out_blocks = [
         o.rearrange("(g n) (ti tj) h d -> g (n ti) (tj h d)", g=4, tj=8) for o in (out_0, out_1, out_2)
@@ -38,9 +38,9 @@ def tile_windowattentionblock_pa_kernel(tc, x, wq, bq, wk, bk, wv, bv, out_0, ou
         perm_a = const.tile([P, P], F32, name="perm_a")
         perm_b = const.tile([P, P], F32, name="perm_b")
         ones = const.tile([P, P], BF16, name="ones")
-        bias_rows = const.tile([P, 2 * F], BF16, name="bias_rows")
+        bias_rows = const.tile([P, 3 * F], BF16, name="bias_rows")
         bias_v_rows = const.tile([P, P], BF16, name="bias_v_rows")
-        bias_all = const.tile([P, 2, F], F32, name="bias_all")
+        bias_all = const.tile([P, 3, F], F32, name="bias_all")
         bias_col = const.tile([P, 4], F32, name="bias_col")
         w_raw = [const.tile([P, 4, F], BF16, name="w_raw%d" % o) for o in range(3)]
         w_grp = [const.tile([P, F, 4], BF16, name="w_grp%d" % o, align_bytes=64) for o in range(3)]
@@ -78,9 +78,10 @@ def tile_windowattentionblock_pa_kernel(tc, x, wq, bq, wk, bk, wv, bv, out_0, ou
         load_x(0, 6 * F, 8 * F)
         load_w(1)
         load_b(1)
-        load_w(2)
-        nc.sync.dma_start(out=bias_v_rows[0:4, :], in_=bv.rearrange("(c h) d -> c (h d)", c=4))
         load_x(0, 0, 4 * F)
+        load_w(2)
+        load_b(2)
+        nc.sync.dma_start(out=bias_v_rows[0:4, :], in_=bv.rearrange("(c h) d -> c (h d)", c=4))
         load_x(1, 0, 8 * F)
         load_x(2, 0, 8 * F)
         load_x(3, 0, 8 * F)
@@ -92,12 +93,12 @@ def tile_windowattentionblock_pa_kernel(tc, x, wq, bq, wk, bk, wv, bv, out_0, ou
         nc.vector.tensor_copy(out=dst_b[:, :, 7:8, :], in_=src[:, :, 0:1, :])
 
         def spread_bias(o):
-            bank = psum.tile([P, F], F32, tag="at", bufs=2, name="bank")
+            bank = psum.tile([P, F], F32, tag="s", bufs=4, name="bank")
             nc.tensor.matmul(out=bank[:], lhsT=ones[:], rhs=bias_rows[:, o * F : (o + 1) * F], start=True, stop=True)
             nc.scalar.copy(out=bias_all[:, o, :], in_=bank[:])
 
         def stand_bias_v():
-            bank = psum.tile([P, F], F32, tag="at", bufs=2, name="bank")
+            bank = psum.tile([P, F], F32, tag="s", bufs=4, name="bank")
             nc.tensor.matmul(out=bank[:, 0:32], lhsT=bias_v_rows[:], rhs=ident_bf[:, 0:32], start=True, stop=True)
             nc.scalar.copy(out=bias_col[:], in_=bank[:, 0:4])
 
@@ -127,7 +128,7 @@ def tile_windowattentionblock_pa_kernel(tc, x, wq, bq, wk, bk, wv, bv, out_0, ou
                 grouped[g] = xq.tile([P, 4 * F], BF16, tag="gx", name="gx", align_bytes=64)
             gw = grouped[g][:].bitcast(F32)
             for b in pairs:
-                xt = psum.tile([P, F], F32, tag="t", bufs=3, name="xt")
+                xt = psum.tile([P, F], F32, tag="s", bufs=4, name="xt")
                 for s in range(2):
                     cl = (4 if half == 0 else 0) + 2 * b + s
                     for u in range(2):
@@ -141,8 +142,8 @@ def tile_windowattentionblock_pa_kernel(tc, x, wq, bq, wk, bk, wv, bv, out_0, ou
 
         def quant_x(g, s0=0, s1=4):
             if s0 == 0:
-                codes = xq.tile([P, F], U32, tag="xc", name="codes", align_bytes=64)
-                scales = xq.tile([P, F], U8, tag="xs", name="scales", align_bytes=64)
+                codes = xq.tile([P, F], U32, tag="xc", name="codes", align_bytes=64, bufs=3)
+                scales = xq.tile([P, F], U8, tag="xs", name="scales", align_bytes=64, bufs=3)
                 packed[g] = (codes, scales)
             codes, scales = packed[g]
             nc.vector.quantize_mx(
@@ -163,7 +164,7 @@ def tile_windowattentionblock_pa_kernel(tc, x, wq, bq, wk, bk, wv, bv, out_0, ou
                 staged[(g, o)] = stage.tile([P, 4 * F], F32, tag="st%d" % o, name="st%d" % o)
             codes, scales = packed[g]
             cols = slice(s * P, (s + 1) * P)
-            acc = psum.tile([P, F], F32, tag="av", bufs=3, name="acc_v")
+            acc = psum.tile([P, F], F32, tag="v", bufs=4, name="acc_v")
             nc.tensor.matmul_mx(
                 out=acc[:],
                 lhsT=codes[:, cols].bitcast(FP8X4),
@@ -182,7 +183,7 @@ def tile_windowattentionblock_pa_kernel(tc, x, wq, bq, wk, bk, wv, bv, out_0, ou
         def channel_bank(g, c):
             codes, scales = packed[g]
             cols = slice(c * P, (c + 1) * P)
-            acc = psum.tile([P, F], F32, tag="at", bufs=2, name="acc_t")
+            acc = psum.tile([P, F], F32, tag="s", bufs=4, name="acc_t")
             nc.tensor.matmul_mx(
                 out=acc[:],
                 lhsT=w_codes[2][:, cols].bitcast(FP8X4),
@@ -199,7 +200,7 @@ def tile_windowattentionblock_pa_kernel(tc, x, wq, bq, wk, bk, wv, bv, out_0, ou
         def flip_back(g, s, engine_copy):
             if s == 0:
                 staged[(g, 2)] = stage.tile([P, 4 * F], F32, tag="st2", name="st2")
-            bank = psum.tile([P, F], F32, tag="t", bufs=3, name="bk")
+            bank = psum.tile([P, F], F32, tag="s", bufs=4, name="bk")
             for c in range(4):
                 nc.tensor.transpose(bank[:, c * P : (c + 1) * P], flipped[(g, c)][:, s * P : (s + 1) * P], ident[:])
             engine_copy(out=staged[(g, 2)][:, s * F : (s + 1) * F], in_=bank[:])
@@ -212,42 +213,38 @@ def tile_windowattentionblock_pa_kernel(tc, x, wq, bq, wk, bk, wv, bv, out_0, ou
         quant_x(0, 0, 2)
         quant_x(0, 2, 4)
         regroup_w(1, nc.scalar.copy)
-        for s in range(4):
-            vector_bank(0, 0, s)
         spread_bias(1)
-        transposes(1)
+        for s in range(3):
+            vector_bank(0, 0, s)
         quant_w(1)
-        for s in range(4):
+        vector_bank(0, 0, 3)
+        transposes(1)
+        for s in range(3):
             vector_bank(0, 1, s)
+        quant_x(1)
+        vector_bank(0, 1, 3)
         regroup_w(2, nc.scalar.copy)
         stand_bias_v()
-        quant_x(1)
         quant_w(2)
-        for c in range(4):
-            channel_bank(0, c)
 
         for g in range(1, 8):
-            vector_bank(g, 0, 0)
-            vector_bank(g, 0, 1)
-            channel_bank(g, 0)
-            vector_bank(g, 0, 2)
-            channel_bank(g, 1)
-            vector_bank(g, 0, 3)
+            for s in range(4):
+                vector_bank(g, 0, s)
+                channel_bank(g - 1, s)
             if g < 7:
                 transposes(g + 1)
-            flip_back(g - 1, 0, nc.scalar.copy)
             vector_bank(g, 1, 0)
+            vector_bank(g, 1, 1)
+            flip_back(g - 1, 0, nc.scalar.copy)
+            flip_back(g - 1, 1, nc.scalar.copy)
             if g < 7:
                 quant_x(g + 1)
-            vector_bank(g, 1, 1)
-            channel_bank(g, 2)
             vector_bank(g, 1, 2)
-            channel_bank(g, 3)
             vector_bank(g, 1, 3)
-            for s in range(1, 4):
-                flip_back(g - 1, s, nc.scalar.copy)
+            flip_back(g - 1, 2, nc.scalar.copy)
+            flip_back(g - 1, 3, nc.scalar.copy)
             store(g - 1, 2, 0, 4)
+            if g == 5:
+                spread_bias(2)
         for s in range(4):
-            flip_back(7, s, nc.vector.tensor_copy if s % 2 == 0 else nc.scalar.copy)
-            if s % 2 == 1:
-                store(7, 2, s - 1, s + 1)
+            vector_bank(7, 2, s)

@@ -225,24 +225,28 @@ def tile_windowattentionblock_pa_kernel(tc, x, wq, bq, wk, bk, wv, bv, out_0, ou
         vector_bank(0, 1, 3)
         regroup_w(2, nc.scalar.copy)
         stand_bias_v()
+        transposes(2)
         quant_w(2)
 
         for g in range(1, 8):
-            for s in range(4):
-                vector_bank(g, 0, s)
-                channel_bank(g - 1, s)
-            if g < 7:
-                transposes(g + 1)
+            vector_bank(g, 0, 0)
+            vector_bank(g, 0, 1)
+            channel_bank(g - 1, 0)
+            vector_bank(g, 0, 2)
+            channel_bank(g - 1, 1)
+            vector_bank(g, 0, 3)
+            channel_bank(g - 1, 2)
             vector_bank(g, 1, 0)
+            channel_bank(g - 1, 3)
             vector_bank(g, 1, 1)
-            flip_back(g - 1, 0, nc.scalar.copy)
-            flip_back(g - 1, 1, nc.scalar.copy)
+            vector_bank(g, 1, 2)
             if g < 7:
                 quant_x(g + 1)
-            vector_bank(g, 1, 2)
             vector_bank(g, 1, 3)
-            flip_back(g - 1, 2, nc.scalar.copy)
-            flip_back(g - 1, 3, nc.scalar.copy)
+            if g < 6:
+                transposes(g + 2)
+            for s in range(4):
+                flip_back(g - 1, s, nc.scalar.copy)
             store(g - 1, 2, 0, 4)
             if g == 5:
                 spread_bias(2)

@@ -175,7 +175,7 @@ def tile_windowattentionblock_pa_kernel(tc, x, wq, bq, wk, bk, wv, bv, out_0, ou
                 stop=True,
             )
             nc.vector.tensor_tensor(
-                out=staged[(g, o)][:, s * F : (s + 1) * F], in0=acc[:], in1=bias_all[:, o, :], op=ADD
+                out=staged[(g, o)][:, s * F : (s + 1) * F], in0=bias_all[:, o, :], in1=acc[:], op=ADD
             )
             if s == 3:
                 store(g, o, 0, 4)

@@ -9,7 +9,6 @@ U32 = mybir.dt.uint32
 U8 = mybir.dt.uint8
 FP8X4 = mybir.dt.float8_e4m3fn_x4
 ADD = mybir.AluOpType.add
-IDENTITY = mybir.ActivationFunctionType.Identity
 
 P = 128
 F = 512
@@ -28,20 +27,16 @@ def tile_windowattentionblock_pa_kernel(tc, x, wq, bq, wk, bk, wv, bv, out_0, ou
     with ExitStack() as ctx:
         const = ctx.enter_context(tc.tile_pool(name="const", bufs=1))
         xq = ctx.enter_context(tc.tile_pool(name="xq", bufs=2))
-        flip = ctx.enter_context(tc.tile_pool(name="flip", bufs=2))
         stage = ctx.enter_context(tc.tile_pool(name="stage", bufs=5))
         psum = ctx.enter_context(tc.psum_pool(name="psum", bufs=1))
         ctx.enter_context(tc.manual_schedule())
 
         ident = const.tile([P, P], F32, name="ident")
-        ident_bf = const.tile([P, P], BF16, name="ident_bf")
         perm_a = const.tile([P, P], F32, name="perm_a")
         perm_b = const.tile([P, P], F32, name="perm_b")
         ones = const.tile([P, P], BF16, name="ones")
         bias_rows = const.tile([P, 3 * F], BF16, name="bias_rows")
-        bias_v_rows = const.tile([P, P], BF16, name="bias_v_rows")
         bias_all = const.tile([P, 3, F], F32, name="bias_all")
-        bias_col = const.tile([P, 4], F32, name="bias_col")
         w_raw = [const.tile([P, 4, F], BF16, name="w_raw%d" % o) for o in range(3)]
         w_grp = [const.tile([P, F, 4], BF16, name="w_grp%d" % o, align_bytes=64) for o in range(3)]
         w_codes = [const.tile([P, F], U32, name="w_codes%d" % o, align_bytes=64) for o in range(3)]
@@ -67,10 +62,8 @@ def tile_windowattentionblock_pa_kernel(tc, x, wq, bq, wk, bk, wv, bv, out_0, ou
                 nc.sync.dma_start(out=x_sb[blk][n:P, c0:c1], in_=x_rows[0 : P - n, c0:c1])
 
         nc.vector.memset(bias_rows[:].bitcast(F32), 0.0)
-        nc.vector.memset(bias_v_rows[:].bitcast(F32), 0.0)
         nc.vector.memset(ones[:], 1.0)
         make_identity(nc, ident[:])
-        make_identity(nc, ident_bf[:])
 
         load_w(0)
         load_b(0)
@@ -81,7 +74,6 @@ def tile_windowattentionblock_pa_kernel(tc, x, wq, bq, wk, bk, wv, bv, out_0, ou
         load_x(0, 0, 4 * F)
         load_w(2)
         load_b(2)
-        nc.sync.dma_start(out=bias_v_rows[0:4, :], in_=bv.rearrange("(c h) d -> c (h d)", c=4))
         load_x(1, 0, 8 * F)
         load_x(2, 0, 8 * F)
         load_x(3, 0, 8 * F)
@@ -96,11 +88,6 @@ def tile_windowattentionblock_pa_kernel(tc, x, wq, bq, wk, bk, wv, bv, out_0, ou
             bank = psum.tile([P, F], F32, tag="s", bufs=4, name="bank")
             nc.tensor.matmul(out=bank[:], lhsT=ones[:], rhs=bias_rows[:, o * F : (o + 1) * F], start=True, stop=True)
             nc.scalar.copy(out=bias_all[:, o, :], in_=bank[:])
-
-        def stand_bias_v():
-            bank = psum.tile([P, F], F32, tag="s", bufs=4, name="bank")
-            nc.tensor.matmul(out=bank[:, 0:32], lhsT=bias_v_rows[:], rhs=ident_bf[:, 0:32], start=True, stop=True)
-            nc.scalar.copy(out=bias_col[:], in_=bank[:, 0:4])
 
         def regroup_w(o, engine_copy):
             engine_copy(
@@ -118,7 +105,6 @@ def tile_windowattentionblock_pa_kernel(tc, x, wq, bq, wk, bk, wv, bv, out_0, ou
         grouped = {}
         packed = {}
         staged = {}
-        flipped = {}
 
         def transposes(g, pairs=(0, 1)):
             blk, half = divmod(g, 2)
@@ -180,30 +166,24 @@ def tile_windowattentionblock_pa_kernel(tc, x, wq, bq, wk, bk, wv, bv, out_0, ou
             if s == 3:
                 store(g, o, 0, 4)
 
-        def channel_bank(g, c):
+        def scalar_bank(g, s):
+            if s == 0:
+                staged[(g, 2)] = stage.tile([P, 4 * F], F32, tag="st2", name="st2")
             codes, scales = packed[g]
-            cols = slice(c * P, (c + 1) * P)
-            acc = psum.tile([P, F], F32, tag="s", bufs=4, name="acc_t")
+            cols = slice(s * P, (s + 1) * P)
+            acc = psum.tile([P, F], F32, tag="s", bufs=4, name="acc_s")
             nc.tensor.matmul_mx(
                 out=acc[:],
-                lhsT=w_codes[2][:, cols].bitcast(FP8X4),
-                lhsT_scale=w_scales[2][:, cols],
-                rhs=codes[:].bitcast(FP8X4),
-                rhs_scale=scales[:],
+                lhsT=codes[:, cols].bitcast(FP8X4),
+                lhsT_scale=scales[:, cols],
+                rhs=w_codes[2][:].bitcast(FP8X4),
+                rhs_scale=w_scales[2][:],
                 start=True,
                 stop=True,
             )
-            vt = flip.tile([P, F], F32, tag="vt%d" % c, name="vt%d" % c)
-            nc.scalar.activation(out=vt[:], in_=acc[:], func=IDENTITY, bias=bias_col[:, c : c + 1], scale=1.0)
-            flipped[(g, c)] = vt
-
-        def flip_back(g, s, engine_copy):
-            if s == 0:
-                staged[(g, 2)] = stage.tile([P, 4 * F], F32, tag="st2", name="st2")
-            bank = psum.tile([P, F], F32, tag="s", bufs=4, name="bk")
-            for c in range(4):
-                nc.tensor.transpose(bank[:, c * P : (c + 1) * P], flipped[(g, c)][:, s * P : (s + 1) * P], ident[:])
-            engine_copy(out=staged[(g, 2)][:, s * F : (s + 1) * F], in_=bank[:])
+            part = staged[(g, 2)][:, s * F : (s + 1) * F]
+            nc.scalar.copy(out=part, in_=acc[:])
+            nc.gpsimd.tensor_tensor(out=part, in0=part, in1=bias_all[:, 2, :], op=ADD)
 
         spread_bias(0)
         transposes(0, (0,))
@@ -224,31 +204,27 @@ def tile_windowattentionblock_pa_kernel(tc, x, wq, bq, wk, bk, wv, bv, out_0, ou
         quant_x(1)
         vector_bank(0, 1, 3)
         regroup_w(2, nc.scalar.copy)
-        stand_bias_v()
+        spread_bias(2)
         transposes(2)
         quant_w(2)
 
         for g in range(1, 8):
             vector_bank(g, 0, 0)
             vector_bank(g, 0, 1)
-            channel_bank(g - 1, 0)
+            scalar_bank(g - 1, 0)
             vector_bank(g, 0, 2)
-            channel_bank(g - 1, 1)
+            scalar_bank(g - 1, 1)
             vector_bank(g, 0, 3)
-            channel_bank(g - 1, 2)
+            scalar_bank(g - 1, 2)
             vector_bank(g, 1, 0)
-            channel_bank(g - 1, 3)
+            scalar_bank(g - 1, 3)
             vector_bank(g, 1, 1)
             vector_bank(g, 1, 2)
             if g < 7:
                 quant_x(g + 1)
             vector_bank(g, 1, 3)
+            store(g - 1, 2, 0, 4)
             if g < 6:
                 transposes(g + 2)
-            for s in range(4):
-                flip_back(g - 1, s, nc.scalar.copy)
-            store(g - 1, 2, 0, 4)
-            if g == 5:
-                spread_bias(2)
         for s in range(4):
             vector_bank(7, 2, s)

@@ -54,12 +54,12 @@ def tile_windowattentionblock_pa_kernel(tc, x, wq, bq, wk, bk, wv, bv, out_0, ou
                 out=bias_rows[0:1, o * F : (o + 1) * F], in_=biases[o].rearrange("(o h) d -> o (h d)", o=1)
             )
 
-        def load_x(blk, c0, c1):
+        def load_x(blk, c0, c1, queue):
             r0 = (16 * blk + 4) * 8
             n = min(P, 512 - r0)
-            nc.sync.dma_start(out=x_sb[blk][0:n, c0:c1], in_=x_rows[r0 : r0 + n, c0:c1])
+            queue.dma_start(out=x_sb[blk][0:n, c0:c1], in_=x_rows[r0 : r0 + n, c0:c1])
             if n < P:
-                nc.sync.dma_start(out=x_sb[blk][n:P, c0:c1], in_=x_rows[0 : P - n, c0:c1])
+                queue.dma_start(out=x_sb[blk][n:P, c0:c1], in_=x_rows[0 : P - n, c0:c1])
 
         nc.vector.memset(bias_rows[:].bitcast(F32), 0.0)
         nc.vector.memset(ones[:], 1.0)
@@ -67,16 +67,14 @@ def tile_windowattentionblock_pa_kernel(tc, x, wq, bq, wk, bk, wv, bv, out_0, ou
 
         load_w(0)
         load_b(0)
-        load_x(0, 4 * F, 6 * F)
-        load_x(0, 6 * F, 8 * F)
+        load_x(0, 4 * F, 6 * F, nc.sync)
+        load_x(0, 6 * F, 8 * F, nc.sync)
         load_w(1)
         load_b(1)
-        load_x(0, 0, 4 * F)
+        load_x(0, 0, 4 * F, nc.sync)
         load_w(2)
         load_b(2)
-        load_x(1, 0, 8 * F)
-        load_x(2, 0, 8 * F)
-        load_x(3, 0, 8 * F)
+        load_x(1, 0, 8 * F, nc.sync)
 
         src = ident[:].rearrange("k (a t g) -> k a g t", a=2, t=8, g=8)
         nc.vector.tensor_copy(out=perm_a[:].rearrange("k (a g t) -> k a g t", a=2, g=8, t=8), in_=src)
@@ -138,10 +136,10 @@ def tile_windowattentionblock_pa_kernel(tc, x, wq, bq, wk, bk, wv, bv, out_0, ou
                 in_=grouped[g][:, s0 * F : s1 * F],
             )
 
-        def store(g, o, s0, s1):
+        def store(g, o, s0, s1, queue):
             blk, half = divmod(g, 2)
             c0 = half * 4 * F
-            nc.sync.dma_start(
+            queue.dma_start(
                 out=out_blocks[o][blk][:, c0 + s0 * F : c0 + s1 * F], in_=staged[(g, o)][:, s0 * F : s1 * F]
             )
 
@@ -163,8 +161,8 @@ def tile_windowattentionblock_pa_kernel(tc, x, wq, bq, wk, bk, wv, bv, out_0, ou
             nc.vector.tensor_tensor(
                 out=staged[(g, o)][:, s * F : (s + 1) * F], in0=bias_all[:, o, :], in1=acc[:], op=ADD
             )
-            if s == 3:
-                store(g, o, 0, 4)
+            if s == 3 and (o != 1 or g < 2):
+                store(g, o, 0, 4, nc.sync)
 
         def scalar_bank(g, s):
             if s == 0:
@@ -193,6 +191,8 @@ def tile_windowattentionblock_pa_kernel(tc, x, wq, bq, wk, bk, wv, bv, out_0, ou
         quant_x(0, 0, 2)
         quant_x(0, 2, 4)
         regroup_w(1, nc.scalar.copy)
+        load_x(2, 0, 8 * F, nc.scalar)
+        load_x(3, 0, 8 * F, nc.scalar)
         spread_bias(1)
         for s in range(3):
             vector_bank(0, 0, s)
@@ -214,6 +214,10 @@ def tile_windowattentionblock_pa_kernel(tc, x, wq, bq, wk, bk, wv, bv, out_0, ou
             scalar_bank(g - 1, 0)
             vector_bank(g, 0, 2)
             scalar_bank(g - 1, 1)
+            if g > 2:
+                store(g - 1, 1, 0, 4, nc.scalar)
+            if g % 2 == 1 and g > 1:
+                store(g - 2, 2, 0, 4, nc.scalar)
             vector_bank(g, 0, 3)
             scalar_bank(g - 1, 2)
             vector_bank(g, 1, 0)
@@ -223,8 +227,10 @@ def tile_windowattentionblock_pa_kernel(tc, x, wq, bq, wk, bk, wv, bv, out_0, ou
             if g < 7:
                 quant_x(g + 1)
             vector_bank(g, 1, 3)
-            store(g - 1, 2, 0, 4)
+            if g % 2 == 1:
+                store(g - 1, 2, 0, 4, nc.sync)
             if g < 6:
                 transposes(g + 2)
+        store(7, 1, 0, 4, nc.scalar)
         for s in range(4):
             vector_bank(7, 2, s)

from contextlib import ExitStack

import concourse.mybir as mybir
from concourse.masks import make_identity

F32 = mybir.dt.float32
BF16 = mybir.dt.bfloat16
U32 = mybir.dt.uint32
U8 = mybir.dt.uint8
FP8X4 = mybir.dt.float8_e4m3fn_x4
ADD = mybir.AluOpType.add

P = 128
F = 512
FLOPS = 2 * 4096 * 512 * 1536


def tile_windowattentionblock_pa_kernel(tc, x, wq, bq, wk, bk, wv, bv, out_0, out_1, out_2):
    nc = tc.nc
    weights = (wq, wk, wv)
    biases = (bq, bk, bv)
    x_rows = x.rearrange("b r (cb cl) c -> (b r cb) (cl c)", cl=8)
    out_blocks = [
        o.rearrange("(g n) (ti tj) h d -> g (n ti) (tj h d)", g=4, tj=8) for o in (out_0, out_1, out_2)
    ]

    with ExitStack() as ctx:
        const = ctx.enter_context(tc.tile_pool(name="const", bufs=1))
        xq = ctx.enter_context(tc.tile_pool(name="xq", bufs=2))
        stage = ctx.enter_context(tc.tile_pool(name="stage", bufs=5))
        psum = ctx.enter_context(tc.psum_pool(name="psum", bufs=1))
        ctx.enter_context(tc.manual_schedule())

        ident = const.tile([P, P], F32, name="ident")
        perm_a = const.tile([P, P], F32, name="perm_a")
        perm_b = const.tile([P, P], F32, name="perm_b")
        ones = const.tile([P, P], BF16, name="ones")
        bias_rows = const.tile([P, 3 * F], BF16, name="bias_rows")
        bias_all = const.tile([P, 3, F], F32, name="bias_all")
        w_raw = [const.tile([P, 4, F], BF16, name="w_raw%d" % o) for o in range(3)]
        w_grp = [const.tile([P, F, 4], BF16, name="w_grp%d" % o, align_bytes=64) for o in range(3)]
        w_codes = [const.tile([P, F], U32, name="w_codes%d" % o, align_bytes=64) for o in range(3)]
        w_scales = [const.tile([P, F], U8, name="w_scales%d" % o, align_bytes=64) for o in range(3)]
        x_sb = [const.tile([P, 8 * F], BF16, name="x_sb%d" % g) for g in range(4)]

        def load_w(o):
            nc.sync.dma_start(
                out=w_raw[o][:].rearrange("q t f -> q (t f)"),
                in_=weights[o].rearrange("(q t) h d -> q (t h d)", t=4),
            )

        def load_b(o):
            nc.sync.dma_start(
                out=bias_rows[0:1, o * F : (o + 1) * F], in_=biases[o].rearrange("(o h) d -> o (h d)", o=1)
            )

        def load_x(blk, c0, c1, queue):
            r0 = (16 * blk + 4) * 8
            n = min(P, 512 - r0)
            queue.dma_start(out=x_sb[blk][0:n, c0:c1], in_=x_rows[r0 : r0 + n, c0:c1])
            if n < P:
                queue.dma_start(out=x_sb[blk][n:P, c0:c1], in_=x_rows[0 : P - n, c0:c1])

        nc.vector.memset(bias_rows[:].bitcast(F32), 0.0)
        nc.vector.memset(ones[:], 1.0)
        make_identity(nc, ident[:])

        load_w(0)
        load_b(0)
        load_x(0, 4 * F, 6 * F, nc.sync)
        load_x(0, 6 * F, 8 * F, nc.sync)
        load_w(1)
        load_b(1)
        load_x(0, 0, 4 * F, nc.sync)
        load_w(2)
        load_b(2)
        load_x(1, 0, 8 * F, nc.sync)

        src = ident[:].rearrange("k (a t g) -> k a g t", a=2, t=8, g=8)
        nc.vector.tensor_copy(out=perm_a[:].rearrange("k (a g t) -> k a g t", a=2, g=8, t=8), in_=src)
        dst_b = perm_b[:].rearrange("k (a g t) -> k a g t", a=2, g=8, t=8)
        nc.vector.tensor_copy(out=dst_b[:, :, 0:7, :], in_=src[:, :, 1:8, :])
        nc.vector.tensor_copy(out=dst_b[:, :, 7:8, :], in_=src[:, :, 0:1, :])

        def spread_bias(o):
            bank = psum.tile([P, F], F32, tag="s", bufs=4, name="bank")
            nc.tensor.matmul(out=bank[:], lhsT=ones[:], rhs=bias_rows[:, o * F : (o + 1) * F], start=True, stop=True)
            nc.scalar.copy(out=bias_all[:, o, :], in_=bank[:])

        def regroup_w(o, engine_copy):
            engine_copy(
                out=w_grp[o][:].rearrange("p (c i) t -> p c t i", i=4),
                in_=w_raw[o][:].rearrange("p t (c i) -> p c t i", i=4),
            )

        def quant_w(o):
            nc.vector.quantize_mx(
                out=w_codes[o][:].bitcast(FP8X4),
                scales=w_scales[o][:],
                in_=w_grp[o][:].rearrange("p f t -> p (f t)"),
            )

        grouped = {}
        packed = {}
        staged = {}

        def transposes(g, pairs=(0, 1)):
            blk, half = divmod(g, 2)
            perm = perm_a if half == 0 else perm_b
            words = x_sb[blk][:].bitcast(F32)
            if 0 in pairs:
                grouped[g] = xq.tile([P, 4 * F], BF16, tag="gx", name="gx", align_bytes=64)
            gw = grouped[g][:].bitcast(F32)
            for b in pairs:
                xt = psum.tile([P, F], F32, tag="s", bufs=4, name="xt")
                for s in range(2):
                    cl = (4 if half == 0 else 0) + 2 * b + s
                    for u in range(2):
                        j = 2 * s + u
                        c0 = cl * 256 + u
                        nc.tensor.transpose(xt[:, j * P : (j + 1) * P], words[:, c0 : c0 + 255 : 2], perm[:])
                nc.scalar.copy(
                    out=gw[:, b * F : (b + 1) * F].rearrange("p (s n u) -> p s n u", s=2, u=2),
                    in_=xt[:].rearrange("p (s u n) -> p s n u", s=2, u=2),
                )

        def quant_x(g, s0=0, s1=4):
            if s0 == 0:
                codes = xq.tile([P, F], U32, tag="xc", name="codes", align_bytes=64, bufs=3)
                scales = xq.tile([P, F], U8, tag="xs", name="scales", align_bytes=64, bufs=3)
                packed[g] = (codes, scales)
            codes, scales = packed[g]
            nc.vector.quantize_mx(
                out=codes[:, s0 * P : s1 * P].bitcast(FP8X4),
                scales=scales[:, s0 * P : s1 * P],
                in_=grouped[g][:, s0 * F : s1 * F],
            )

        def store(g, o, s0, s1, queue):
            blk, half = divmod(g, 2)
            c0 = half * 4 * F
            queue.dma_start(
                out=out_blocks[o][blk][:, c0 + s0 * F : c0 + s1 * F], in_=staged[(g, o)][:, s0 * F : s1 * F]
            )

        def vector_bank(g, o, s):
            if s == 0:
                staged[(g, o)] = stage.tile([P, 4 * F], F32, tag="st%d" % o, name="st%d" % o)
            codes, scales = packed[g]
            cols = slice(s * P, (s + 1) * P)
            acc = psum.tile([P, F], F32, tag="v", bufs=4, name="acc_v")
            nc.tensor.matmul_mx(
                out=acc[:],
                lhsT=codes[:, cols].bitcast(FP8X4),
                lhsT_scale=scales[:, cols],
                rhs=w_codes[o][:].bitcast(FP8X4),
                rhs_scale=w_scales[o][:],
                start=True,
                stop=True,
            )
            nc.vector.tensor_tensor(
                out=staged[(g, o)][:, s * F : (s + 1) * F], in0=bias_all[:, o, :], in1=acc[:], op=ADD
            )
            if s == 3 and (o != 1 or g < 2):
                store(g, o, 0, 4, nc.sync)

        def scalar_bank(g, s):
            if s == 0:
                staged[(g, 2)] = stage.tile([P, 4 * F], F32, tag="st2", name="st2")
            codes, scales = packed[g]
            cols = slice(s * P, (s + 1) * P)
            acc = psum.tile([P, F], F32, tag="s", bufs=4, name="acc_s")
            nc.tensor.matmul_mx(
                out=acc[:],
                lhsT=codes[:, cols].bitcast(FP8X4),
                lhsT_scale=scales[:, cols],
                rhs=w_codes[2][:].bitcast(FP8X4),
                rhs_scale=w_scales[2][:],
                start=True,
                stop=True,
            )
            part = staged[(g, 2)][:, s * F : (s + 1) * F]
            nc.scalar.copy(out=part, in_=acc[:])
            nc.gpsimd.tensor_tensor(out=part, in0=part, in1=bias_all[:, 2, :], op=ADD)

        spread_bias(0)
        transposes(0, (0,))
        transposes(0, (1,))
        regroup_w(0, nc.vector.tensor_copy)
        quant_w(0)
        quant_x(0, 0, 2)
        quant_x(0, 2, 4)
        regroup_w(1, nc.scalar.copy)
        load_x(2, 0, 8 * F, nc.scalar)
        load_x(3, 0, 8 * F, nc.scalar)
        spread_bias(1)
        for s in range(3):
            vector_bank(0, 0, s)
        quant_w(1)
        vector_bank(0, 0, 3)
        transposes(1)
        for s in range(3):
            vector_bank(0, 1, s)
        quant_x(1)
        vector_bank(0, 1, 3)
        regroup_w(2, nc.scalar.copy)
        spread_bias(2)
        transposes(2)
        quant_w(2)

        for g in range(1, 8):
            vector_bank(g, 0, 0)
            vector_bank(g, 0, 1)
            scalar_bank(g - 1, 0)
            vector_bank(g, 0, 2)
            scalar_bank(g - 1, 1)
            if g > 2:
                store(g - 1, 1, 0, 4, nc.scalar)
            if g % 2 == 1 and g > 1:
                store(g - 2, 2, 0, 4, nc.scalar)
            vector_bank(g, 0, 3)
            scalar_bank(g - 1, 2)
            vector_bank(g, 1, 0)
            scalar_bank(g - 1, 3)
            vector_bank(g, 1, 1)
            vector_bank(g, 1, 2)
            if g < 7:
                quant_x(g + 1)
            vector_bank(g, 1, 3)
            if g % 2 == 1:
                store(g - 1, 2, 0, 4, nc.sync)
            if g < 6:
                transposes(g + 2)
        store(7, 1, 0, 4, nc.scalar)
        for s in range(4):
            vector_bank(7, 2, s)
